import numpy as np
import ml_dtypes


def mxq(x, axis, fmt="e4m3"):
    dtype, down = {"e4m3": (ml_dtypes.float8_e4m3fn, 7), "e5m2": (ml_dtypes.float8_e5m2, 14)}[fmt]
    v = np.moveaxis(np.asarray(x, np.float32).astype(ml_dtypes.bfloat16).astype(np.float64), axis, -1)
    blocks = v.reshape(v.shape[:-1] + (-1, 32))
    amax = np.abs(blocks).max(-1, keepdims=True)
    byte = np.maximum(np.where(amax > 0, np.frexp(amax)[1] - 1 + 127, 0) - down, 1)
    scale = np.exp2(byte - 127.0)
    codes = (blocks / scale).astype(np.float32).astype(dtype).astype(np.float64)
    return np.moveaxis((codes * scale).reshape(v.shape), -1, axis)


WIDE = False


def mx_kscale(k):
    if not WIDE:
        return np.ones(k)
    levels = np.array([10, -10, 5, -5, 0])
    a = np.random.permutation(np.resize(levels, k // 512 * 4)).reshape(k // 512, 4)
    idx = np.arange(k)
    return np.exp2(a[idx // 512, idx % 128 // 32])


BF16 = ml_dtypes.bfloat16


def bf(x):
    return np.asarray(x, np.float32).astype(BF16)


def f64(x):
    return np.asarray(x).astype(np.float64)


M, P, D = 512, 16384, 256


def setup_inputs():
    s = mx_kscale(P)
    return {"G": bf(np.exp(-np.abs(3.0 + np.random.standard_normal((M, P)))) * s[None, :]),
            "x_next": bf(np.random.standard_normal((P, D)) * 1.5 * (s.mean() / s)[:, None])}


def reference(G, x_next):
    g = f64(G)
    p = g / np.sum(g, axis=1, keepdims=True)
    return mxq(p, 1, "e4m3") @ mxq(f64(x_next), 0, "e4m3")

@@ -1,0 +1,231 @@
+from contextlib import ExitStack
+
+import concourse.mybir as mybir
+from concourse.masks import make_identity
+
+F32 = mybir.dt.float32
+BF16 = mybir.dt.bfloat16
+U32 = mybir.dt.uint32
+U8 = mybir.dt.uint8
+FP8X4 = mybir.dt.float8_e4m3fn_x4
+MULT = mybir.AluOpType.mult
+ADD = mybir.AluOpType.add
+COPY = mybir.ActivationFunctionType.Copy
+AXIS_X = mybir.AxisListType.X
+
+P = 128
+PACK = 4
+K_PASS = P * PACK
+ROWS, K, D = 512, 16384, 256
+ROW_BLOCKS = ROWS // P
+PASSES = K // K_PASS
+
+G_CHUNK_PASSES = 8
+G_CHUNK_COLS = G_CHUNK_PASSES * K_PASS
+G_CHUNKS = K // G_CHUNK_COLS
+X_CHUNK_PASSES = 4
+X_CHUNKS = PASSES // X_CHUNK_PASSES
+BANK_PASSES = 2
+BANK_WORDS = 512
+
+CHUNKS = ROW_BLOCKS * G_CHUNKS
+BANKS = G_CHUNK_PASSES // BANK_PASSES
+
+VECTOR_SUM_COLS_BESIDE_X = 1024
+VECTOR_SUM_COLS = 2688
+SUM_SLOTS = 8
+
+LOAD_LEAD = 9
+SUM_LEAD = 6
+
+FLOPS = 2 * ROWS * K * D
+
+
+def tile_nntransformlearner_pb_k_kernel(tc, G, x_next, out):
+    nc = tc.nc
+    with ExitStack() as stack:
+        const = stack.enter_context(tc.tile_pool(name="const", bufs=1))
+        g_pool = stack.enter_context(tc.tile_pool(name="g", bufs=12))
+        x_raw_pool = stack.enter_context(tc.tile_pool(name="x_raw", bufs=4))
+        x_grouped_pool = stack.enter_context(tc.tile_pool(name="x_grouped", bufs=2))
+        p_grouped_pool = stack.enter_context(tc.tile_pool(name="p_grouped", bufs=3))
+        p_mx_pool = stack.enter_context(tc.tile_pool(name="p_mx", bufs=3))
+        result_pool = stack.enter_context(tc.tile_pool(name="result", bufs=2))
+        turned_pool = stack.enter_context(tc.psum_pool(name="turned", bufs=6))
+        acc_pool = stack.enter_context(tc.psum_pool(name="acc", bufs=2))
+        stack.enter_context(tc.manual_schedule())
+
+        identity = const.tile([P, P], F32, name="identity")
+        make_identity(nc, identity[:])
+        partial_sums = const.tile([P, ROW_BLOCKS, 2 * SUM_SLOTS], F32, name="partial_sums")
+        nc.vector.memset(partial_sums[:], 0.0)
+        row_sum = const.tile([P, ROW_BLOCKS], F32, name="row_sum")
+        row_scale = const.tile([P, ROW_BLOCKS], F32, name="row_scale")
+        x_codes = const.tile([P, PASSES * D], U32, name="x_codes", align_bytes=64)
+        x_scales = const.tile([P, PASSES * D], U8, name="x_scales", align_bytes=64)
+
+        x_view = x_next.rearrange("(c q e) d -> q c (e d)", q=P, e=2)
+        g_tiles = {}
+        x_raw_tiles = {}
+        x_grouped_tiles = {}
+        turned_tiles = {}
+        p_grouped_tiles = {}
+        p_mx_tiles = {}
+        acc_tiles = {}
+
+        def load(n):
+            rb, c = divmod(n, G_CHUNKS)
+            g_chunk = g_pool.tile([P, G_CHUNK_COLS], BF16, name="g_chunk")
+            nc.sync.dma_start(
+                out=g_chunk[:],
+                in_=G[rb * P : (rb + 1) * P, c * G_CHUNK_COLS : (c + 1) * G_CHUNK_COLS],
+            )
+            g_tiles[n] = g_chunk
+            if n < X_CHUNKS:
+                x_raw = x_raw_pool.tile([P, X_CHUNK_PASSES * PACK * D], BF16, name="x_raw")
+                halves = 2 * X_CHUNK_PASSES
+                nc.sync.dma_start(
+                    out=x_raw[:].rearrange("p (c r) -> p c r", c=halves),
+                    in_=x_view[:, n * halves : (n + 1) * halves, :],
+                )
+                x_raw_tiles[n] = x_raw
+
+        def sum_rows(n):
+            rb, c = divmod(n, G_CHUNKS)
+            g_chunk = g_tiles[n]
+            split = VECTOR_SUM_COLS_BESIDE_X if n < X_CHUNKS else VECTOR_SUM_COLS
+            nc.vector.tensor_scalar(
+                out=g_chunk[:, :split],
+                in0=g_chunk[:, :split],
+                scalar1=1.0,
+                scalar2=None,
+                op0=MULT,
+                op1=ADD,
+                accum_out=partial_sums[:, rb, c : c + 1],
+            )
+            nc.scalar.activation(
+                out=g_chunk[:, split:],
+                in_=g_chunk[:, split:],
+                func=COPY,
+                accum_out=partial_sums[:, rb, SUM_SLOTS + c : SUM_SLOTS + c + 1],
+            )
+
+        def finish_row_sums(rb):
+            nc.vector.tensor_reduce(
+                out=row_sum[:, rb : rb + 1], in_=partial_sums[:, rb, :], axis=AXIS_X, op=ADD
+            )
+            nc.vector.reciprocal(out=row_scale[:, rb : rb + 1], in_=row_sum[:, rb : rb + 1])
+
+        def regroup_x(j):
+            x_grouped = x_grouped_pool.tile(
+                [P, X_CHUNK_PASSES * D * PACK], BF16, name="x_grouped", align_bytes=64
+            )
+            nc.vector.tensor_copy(
+                out=x_grouped[:].rearrange(
+                    "p (g c i t) -> p g c t i", g=X_CHUNK_PASSES, i=4, t=PACK
+                ),
+                in_=x_raw_tiles[j][:].rearrange(
+                    "p (g t c i) -> p g c t i", g=X_CHUNK_PASSES, i=4, t=PACK
+                ),
+            )
+            x_grouped_tiles[j] = x_grouped
+
+        def quantise_x(j):
+            cols = slice(j * X_CHUNK_PASSES * D, (j + 1) * X_CHUNK_PASSES * D)
+            nc.vector.quantize_mx(
+                out=x_codes[:, cols].bitcast(FP8X4),
+                scales=x_scales[:, cols],
+                in_=x_grouped_tiles[j][:],
+            )
+
+        def scale_rows(n):
+            g_chunk = g_tiles[n]
+            rb = n // G_CHUNKS
+            nc.vector.tensor_scalar(
+                out=g_chunk[:],
+                in0=g_chunk[:],
+                scalar1=row_scale[:, rb : rb + 1],
+                scalar2=None,
+                op0=MULT,
+            )
+
+        def transpose_bank(n, b):
+            p_words = g_tiles[n][:].bitcast(F32)
+            turned = turned_pool.tile([P, BANK_WORDS], F32, name="turned")
+            for s in range(BANK_WORDS // P):
+                w = b * BANK_WORDS + s * P
+                nc.tensor.transpose(
+                    out=turned[:, s * P : (s + 1) * P],
+                    in_=p_words[:, w : w + P],
+                    identity=identity[:],
+                )
+            turned_tiles[(n, b)] = turned
+
+        def copy_bank(n, b):
+            if b == 0:
+                p_grouped_tiles[n] = p_grouped_pool.tile(
+                    [P, G_CHUNK_COLS], BF16, name="p_grouped", align_bytes=64
+                )
+            p_grouped_words = p_grouped_tiles[n][:].bitcast(F32).rearrange(
+                "p (g m u) -> p g m u", g=G_CHUNK_PASSES, u=2
+            )
+            nc.scalar.copy(
+                out=p_grouped_words[:, b * BANK_PASSES : (b + 1) * BANK_PASSES, :, :],
+                in_=turned_tiles[(n, b)][:].rearrange("p (g u m) -> p g m u", g=BANK_PASSES, u=2),
+            )
+
+        def quantise_p(n):
+            p_codes = p_mx_pool.tile([P, G_CHUNK_PASSES * P], U32, name="p_codes", align_bytes=64)
+            p_scales = p_mx_pool.tile([P, G_CHUNK_PASSES * P], U8, name="p_scales", align_bytes=64)
+            nc.vector.quantize_mx(
+                out=p_codes[:].bitcast(FP8X4), scales=p_scales[:], in_=p_grouped_tiles[n][:]
+            )
+            p_mx_tiles[n] = (p_codes, p_scales)
+
+        def multiply(n):
+            rb, c = divmod(n, G_CHUNKS)
+            if c == 0:
+                acc_tiles[rb] = acc_pool.tile([P, D], F32, name="acc")
+            acc = acc_tiles[rb]
+            p_codes, p_scales = p_mx_tiles[n]
+            for i in range(G_CHUNK_PASSES):
+                g = c * G_CHUNK_PASSES + i
+                nc.tensor.matmul_mx(
+                    out=acc[:],
+                    lhsT=p_codes[:, i * P : (i + 1) * P].bitcast(FP8X4),
+                    lhsT_scale=p_scales[:, i * P : (i + 1) * P],
+                    rhs=x_codes[:, g * D : (g + 1) * D].bitcast(FP8X4),
+                    rhs_scale=x_scales[:, g * D : (g + 1) * D],
+                    start=(g == 0),
+                    stop=(g == PASSES - 1),
+                )
+
+        def store(rb):
+            result = result_pool.tile([P, D], F32, name="result")
+            nc.scalar.copy(out=result[:], in_=acc_tiles[rb][:])
+            nc.sync.dma_start(out=out[rb * P : (rb + 1) * P, :], in_=result[:])
+
+        for s in range(-LOAD_LEAD, CHUNKS + 3):
+            if s + LOAD_LEAD < CHUNKS:
+                load(s + LOAD_LEAD)
+            if 0 <= s + 1 < CHUNKS:
+                scale_rows(s + 1)
+            if 0 <= s - 2 < CHUNKS:
+                multiply(s - 2)
+            for b in range(BANKS):
+                if 0 <= s < CHUNKS:
+                    copy_bank(s, b)
+                if 0 <= s + 1 < CHUNKS:
+                    transpose_bank(s + 1, b)
+            if 0 <= s + SUM_LEAD < X_CHUNKS:
+                regroup_x(s + SUM_LEAD)
+            if 0 <= s - 1 < CHUNKS:
+                quantise_p(s - 1)
+            if 0 <= s + SUM_LEAD < CHUNKS:
+                sum_rows(s + SUM_LEAD)
+            if 0 <= s + SUM_LEAD < X_CHUNKS:
+                quantise_x(s + SUM_LEAD)
+            if (s + 2) % G_CHUNKS == 0 and 0 <= s + 2 < CHUNKS:
+                finish_row_sums((s + 2) // G_CHUNKS)
+            if (s - 2) % G_CHUNKS == G_CHUNKS - 1 and 0 <= s - 2 < CHUNKS:
+                store((s - 2) // G_CHUNKS)

@@ -31,12 +31,17 @@ BANK_WORDS = 512
 CHUNKS = ROW_BLOCKS * G_CHUNKS
 BANKS = G_CHUNK_PASSES // BANK_PASSES
 
-VECTOR_SUM_COLS_BESIDE_X = 1024
-VECTOR_SUM_COLS = 2688
+TENSOR_SUM_SLICE = 256
+TENSOR_SUM_COLS = 3 * TENSOR_SUM_SLICE
+VECTOR_SUM_COLS = 2048
+VECTOR_SUM_COLS_BESIDE_X = 512
 SUM_SLOTS = 8
 
-LOAD_LEAD = 9
-SUM_LEAD = 6
+LOAD_LEAD = 6
+SUM_LEAD = 5
+X_CHUNKS_A_STEP = 2
+X_STEPS = X_CHUNKS // X_CHUNKS_A_STEP
+SCALAR_X_PASSES = 2
 
 FLOPS = 2 * ROWS * K * D
 
@@ -51,12 +56,15 @@ def tile_nntransformlearner_pb_k_kernel(tc, G, x_next, out):
         p_grouped_pool = stack.enter_context(tc.tile_pool(name="p_grouped", bufs=3))
         p_mx_pool = stack.enter_context(tc.tile_pool(name="p_mx", bufs=3))
         result_pool = stack.enter_context(tc.tile_pool(name="result", bufs=2))
-        turned_pool = stack.enter_context(tc.psum_pool(name="turned", bufs=6))
+        turned_pool = stack.enter_context(tc.psum_pool(name="turned", bufs=5))
+        sum_pool = stack.enter_context(tc.psum_pool(name="sums", bufs=1))
         acc_pool = stack.enter_context(tc.psum_pool(name="acc", bufs=2))
         stack.enter_context(tc.manual_schedule())
 
         identity = const.tile([P, P], F32, name="identity")
         make_identity(nc, identity[:])
+        identity_bf16 = const.tile([P, P], BF16, name="identity_bf16")
+        make_identity(nc, identity_bf16[:])
         partial_sums = const.tile([P, ROW_BLOCKS, 2 * SUM_SLOTS], F32, name="partial_sums")
         nc.vector.memset(partial_sums[:], 0.0)
         row_sum = const.tile([P, ROW_BLOCKS], F32, name="row_sum")
@@ -72,8 +80,9 @@ def tile_nntransformlearner_pb_k_kernel(tc, G, x_next, out):
         p_grouped_tiles = {}
         p_mx_tiles = {}
         acc_tiles = {}
+        sum_tiles = {}
 
-        def load(n):
+        def load_g(n):
             rb, c = divmod(n, G_CHUNKS)
             g_chunk = g_pool.tile([P, G_CHUNK_COLS], BF16, name="g_chunk")
             nc.sync.dma_start(
@@ -81,19 +90,33 @@ def tile_nntransformlearner_pb_k_kernel(tc, G, x_next, out):
                 in_=G[rb * P : (rb + 1) * P, c * G_CHUNK_COLS : (c + 1) * G_CHUNK_COLS],
             )
             g_tiles[n] = g_chunk
-            if n < X_CHUNKS:
-                x_raw = x_raw_pool.tile([P, X_CHUNK_PASSES * PACK * D], BF16, name="x_raw")
-                halves = 2 * X_CHUNK_PASSES
-                nc.sync.dma_start(
-                    out=x_raw[:].rearrange("p (c r) -> p c r", c=halves),
-                    in_=x_view[:, n * halves : (n + 1) * halves, :],
-                )
-                x_raw_tiles[n] = x_raw
+
+        def load_x(j):
+            x_raw = x_raw_pool.tile([P, X_CHUNK_PASSES * PACK * D], BF16, name="x_raw")
+            halves = 2 * X_CHUNK_PASSES
+            nc.sync.dma_start(
+                out=x_raw[:].rearrange("p (c r) -> p c r", c=halves),
+                in_=x_view[:, j * halves : (j + 1) * halves, :],
+            )
+            x_raw_tiles[j] = x_raw
 
         def sum_rows(n):
             rb, c = divmod(n, G_CHUNKS)
             g_chunk = g_tiles[n]
-            split = VECTOR_SUM_COLS_BESIDE_X if n < X_CHUNKS else VECTOR_SUM_COLS
+            beside_x = 0 <= n - SUM_LEAD < X_STEPS
+            split = VECTOR_SUM_COLS_BESIDE_X if beside_x else VECTOR_SUM_COLS
+            tensor_from = G_CHUNK_COLS - TENSOR_SUM_COLS
+            if c == 0:
+                sum_tiles[rb] = sum_pool.tile([P, TENSOR_SUM_SLICE], F32, name="slice_sums")
+            for i in range(TENSOR_SUM_COLS // TENSOR_SUM_SLICE):
+                first = tensor_from + i * TENSOR_SUM_SLICE
+                nc.tensor.matmul(
+                    out=sum_tiles[rb][:],
+                    lhsT=identity_bf16[:],
+                    rhs=g_chunk[:, first : first + TENSOR_SUM_SLICE],
+                    start=(c == 0 and i == 0),
+                    stop=(c == G_CHUNKS - 1 and first + TENSOR_SUM_SLICE == G_CHUNK_COLS),
+                )
             nc.vector.tensor_scalar(
                 out=g_chunk[:, :split],
                 in0=g_chunk[:, :split],
@@ -104,30 +127,36 @@ def tile_nntransformlearner_pb_k_kernel(tc, G, x_next, out):
                 accum_out=partial_sums[:, rb, c : c + 1],
             )
             nc.scalar.activation(
-                out=g_chunk[:, split:],
-                in_=g_chunk[:, split:],
+                out=g_chunk[:, split:tensor_from],
+                in_=g_chunk[:, split:tensor_from],
                 func=COPY,
                 accum_out=partial_sums[:, rb, SUM_SLOTS + c : SUM_SLOTS + c + 1],
             )
 
         def finish_row_sums(rb):
             nc.vector.tensor_reduce(
+                out=partial_sums[:, rb, G_CHUNKS : G_CHUNKS + 1],
+                in_=sum_tiles[rb][:],
+                axis=AXIS_X,
+                op=ADD,
+            )
+            nc.vector.tensor_reduce(
                 out=row_sum[:, rb : rb + 1], in_=partial_sums[:, rb, :], axis=AXIS_X, op=ADD
             )
             nc.vector.reciprocal(out=row_scale[:, rb : rb + 1], in_=row_sum[:, rb : rb + 1])
 
-        def regroup_x(j):
+        def regroup_x(j, scalar_passes):
             x_grouped = x_grouped_pool.tile(
                 [P, X_CHUNK_PASSES * D * PACK], BF16, name="x_grouped", align_bytes=64
             )
-            nc.vector.tensor_copy(
-                out=x_grouped[:].rearrange(
-                    "p (g c i t) -> p g c t i", g=X_CHUNK_PASSES, i=4, t=PACK
-                ),
-                in_=x_raw_tiles[j][:].rearrange(
-                    "p (g t c i) -> p g c t i", g=X_CHUNK_PASSES, i=4, t=PACK
-                ),
+            to = x_grouped[:].rearrange("p (g c i t) -> p g c t i", g=X_CHUNK_PASSES, i=4, t=PACK)
+            of = x_raw_tiles[j][:].rearrange(
+                "p (g t c i) -> p g c t i", g=X_CHUNK_PASSES, i=4, t=PACK
             )
+            vector_passes = X_CHUNK_PASSES - scalar_passes
+            nc.vector.tensor_copy(out=to[:, :vector_passes], in_=of[:, :vector_passes])
+            for g in range(vector_passes, X_CHUNK_PASSES):
+                nc.scalar.copy(out=to[:, g], in_=of[:, g])
             x_grouped_tiles[j] = x_grouped
 
         def quantise_x(j):
@@ -206,8 +235,14 @@ def tile_nntransformlearner_pb_k_kernel(tc, G, x_next, out):
             nc.sync.dma_start(out=out[rb * P : (rb + 1) * P, :], in_=result[:])
 
         for s in range(-LOAD_LEAD, CHUNKS + 3):
+            prepares_x = 0 <= s < X_STEPS
+            if 0 <= s + 1 < X_STEPS:
+                load_x(X_CHUNKS_A_STEP * (s + 1))
+                load_x(X_CHUNKS_A_STEP * (s + 1) + 1)
             if s + LOAD_LEAD < CHUNKS:
-                load(s + LOAD_LEAD)
+                load_g(s + LOAD_LEAD)
+            if (s + 1) % G_CHUNKS == 0 and 0 <= s + 1 < CHUNKS:
+                finish_row_sums((s + 1) // G_CHUNKS)
             if 0 <= s + 1 < CHUNKS:
                 scale_rows(s + 1)
             if 0 <= s - 2 < CHUNKS:
@@ -217,15 +252,16 @@ def tile_nntransformlearner_pb_k_kernel(tc, G, x_next, out):
                     copy_bank(s, b)
                 if 0 <= s + 1 < CHUNKS:
                     transpose_bank(s + 1, b)
-            if 0 <= s + SUM_LEAD < X_CHUNKS:
-                regroup_x(s + SUM_LEAD)
+            if prepares_x:
+                regroup_x(X_CHUNKS_A_STEP * s, 0)
             if 0 <= s - 1 < CHUNKS:
                 quantise_p(s - 1)
+            if prepares_x:
+                regroup_x(X_CHUNKS_A_STEP * s + 1, SCALAR_X_PASSES)
+                quantise_x(X_CHUNKS_A_STEP * s)
             if 0 <= s + SUM_LEAD < CHUNKS:
                 sum_rows(s + SUM_LEAD)
-            if 0 <= s + SUM_LEAD < X_CHUNKS:
-                quantise_x(s + SUM_LEAD)
-            if (s + 2) % G_CHUNKS == 0 and 0 <= s + 2 < CHUNKS:
-                finish_row_sums((s + 2) // G_CHUNKS)
+            if prepares_x:
+                quantise_x(X_CHUNKS_A_STEP * s + 1)
             if (s - 2) % G_CHUNKS == G_CHUNKS - 1 and 0 <= s - 2 < CHUNKS:
                 store((s - 2) // G_CHUNKS)

@@ -32,15 +32,15 @@ CHUNKS = ROW_BLOCKS * G_CHUNKS
 BANKS = G_CHUNK_PASSES // BANK_PASSES
 
 TENSOR_SUM_SLICE = 256
-TENSOR_SUM_COLS = 3 * TENSOR_SUM_SLICE
-VECTOR_SUM_COLS = 2048
-VECTOR_SUM_COLS_BESIDE_X = 512
+TENSOR_SUM_COLS = (0, 12 * TENSOR_SUM_SLICE, 0, 0)
+VECTOR_SUM_COLS = (2816, 1024, 2560, 2560)
 SUM_SLOTS = 8
 
 LOAD_LEAD = 6
 SUM_LEAD = 5
 X_CHUNKS_A_STEP = 2
 X_STEPS = X_CHUNKS // X_CHUNKS_A_STEP
+X_FIRST_STEP = -1
 SCALAR_X_PASSES = 2
 
 FLOPS = 2 * ROWS * K * D
@@ -103,12 +103,11 @@ def tile_nntransformlearner_pb_k_kernel(tc, G, x_next, out):
         def sum_rows(n):
             rb, c = divmod(n, G_CHUNKS)
             g_chunk = g_tiles[n]
-            beside_x = 0 <= n - SUM_LEAD < X_STEPS
-            split = VECTOR_SUM_COLS_BESIDE_X if beside_x else VECTOR_SUM_COLS
-            tensor_from = G_CHUNK_COLS - TENSOR_SUM_COLS
-            if c == 0:
+            split = VECTOR_SUM_COLS[rb]
+            tensor_from = G_CHUNK_COLS - TENSOR_SUM_COLS[rb]
+            if c == 0 and TENSOR_SUM_COLS[rb]:
                 sum_tiles[rb] = sum_pool.tile([P, TENSOR_SUM_SLICE], F32, name="slice_sums")
-            for i in range(TENSOR_SUM_COLS // TENSOR_SUM_SLICE):
+            for i in range(TENSOR_SUM_COLS[rb] // TENSOR_SUM_SLICE):
                 first = tensor_from + i * TENSOR_SUM_SLICE
                 nc.tensor.matmul(
                     out=sum_tiles[rb][:],
@@ -126,20 +125,22 @@ def tile_nntransformlearner_pb_k_kernel(tc, G, x_next, out):
                 op1=ADD,
                 accum_out=partial_sums[:, rb, c : c + 1],
             )
-            nc.scalar.activation(
-                out=g_chunk[:, split:tensor_from],
-                in_=g_chunk[:, split:tensor_from],
-                func=COPY,
-                accum_out=partial_sums[:, rb, SUM_SLOTS + c : SUM_SLOTS + c + 1],
-            )
+            if split < tensor_from:
+                nc.scalar.activation(
+                    out=g_chunk[:, split:tensor_from],
+                    in_=g_chunk[:, split:tensor_from],
+                    func=COPY,
+                    accum_out=partial_sums[:, rb, SUM_SLOTS + c : SUM_SLOTS + c + 1],
+                )
 
         def finish_row_sums(rb):
-            nc.vector.tensor_reduce(
-                out=partial_sums[:, rb, G_CHUNKS : G_CHUNKS + 1],
-                in_=sum_tiles[rb][:],
-                axis=AXIS_X,
-                op=ADD,
-            )
+            if TENSOR_SUM_COLS[rb]:
+                nc.vector.tensor_reduce(
+                    out=partial_sums[:, rb, G_CHUNKS : G_CHUNKS + 1],
+                    in_=sum_tiles[rb][:],
+                    axis=AXIS_X,
+                    op=ADD,
+                )
             nc.vector.tensor_reduce(
                 out=row_sum[:, rb : rb + 1], in_=partial_sums[:, rb, :], axis=AXIS_X, op=ADD
             )
@@ -235,10 +236,11 @@ def tile_nntransformlearner_pb_k_kernel(tc, G, x_next, out):
             nc.sync.dma_start(out=out[rb * P : (rb + 1) * P, :], in_=result[:])
 
         for s in range(-LOAD_LEAD, CHUNKS + 3):
-            prepares_x = 0 <= s < X_STEPS
-            if 0 <= s + 1 < X_STEPS:
-                load_x(X_CHUNKS_A_STEP * (s + 1))
-                load_x(X_CHUNKS_A_STEP * (s + 1) + 1)
+            xs = s - X_FIRST_STEP
+            prepares_x = 0 <= xs < X_STEPS
+            if 0 <= xs + 1 < X_STEPS:
+                load_x(X_CHUNKS_A_STEP * (xs + 1))
+                load_x(X_CHUNKS_A_STEP * (xs + 1) + 1)
             if s + LOAD_LEAD < CHUNKS:
                 load_g(s + LOAD_LEAD)
             if (s + 1) % G_CHUNKS == 0 and 0 <= s + 1 < CHUNKS:
@@ -253,15 +255,15 @@ def tile_nntransformlearner_pb_k_kernel(tc, G, x_next, out):
                 if 0 <= s + 1 < CHUNKS:
                     transpose_bank(s + 1, b)
             if prepares_x:
-                regroup_x(X_CHUNKS_A_STEP * s, 0)
+                regroup_x(X_CHUNKS_A_STEP * xs, SCALAR_X_PASSES)
             if 0 <= s - 1 < CHUNKS:
                 quantise_p(s - 1)
             if prepares_x:
-                regroup_x(X_CHUNKS_A_STEP * s + 1, SCALAR_X_PASSES)
-                quantise_x(X_CHUNKS_A_STEP * s)
+                regroup_x(X_CHUNKS_A_STEP * xs + 1, SCALAR_X_PASSES)
+                quantise_x(X_CHUNKS_A_STEP * xs)
             if 0 <= s + SUM_LEAD < CHUNKS:
                 sum_rows(s + SUM_LEAD)
             if prepares_x:
-                quantise_x(X_CHUNKS_A_STEP * s + 1)
+                quantise_x(X_CHUNKS_A_STEP * xs + 1)
             if (s - 2) % G_CHUNKS == G_CHUNKS - 1 and 0 <= s - 2 < CHUNKS:
                 store((s - 2) // G_CHUNKS)

@@ -31,10 +31,15 @@ BANK_WORDS = 512
 CHUNKS = ROW_BLOCKS * G_CHUNKS
 BANKS = G_CHUNK_PASSES // BANK_PASSES
 
-TENSOR_SUM_SLICE = 256
+TENSOR_SUM_SLICE = 272
 TENSOR_SUM_COLS = (0, 12 * TENSOR_SUM_SLICE, 0, 0)
-VECTOR_SUM_COLS = (2816, 1024, 2560, 2560)
+VECTOR_SUM_COLS = (2816, 832, 2688, 2688)
 SUM_SLOTS = 8
+TENSOR_SUM_SLOT = SUM_SLOTS - 1
+
+LAST_PIECES = 4
+PIECE_COLS = G_CHUNK_COLS // LAST_PIECES
+PIECE_VECTOR_COLS = 704
 
 LOAD_LEAD = 6
 SUM_LEAD = 5
@@ -85,10 +90,16 @@ def tile_nntransformlearner_pb_k_kernel(tc, G, x_next, out):
         def load_g(n):
             rb, c = divmod(n, G_CHUNKS)
             g_chunk = g_pool.tile([P, G_CHUNK_COLS], BF16, name="g_chunk")
-            nc.sync.dma_start(
-                out=g_chunk[:],
-                in_=G[rb * P : (rb + 1) * P, c * G_CHUNK_COLS : (c + 1) * G_CHUNK_COLS],
-            )
+            pieces = LAST_PIECES if n == G_CHUNKS - 1 else 1
+            cols = G_CHUNK_COLS // pieces
+            for i in range(pieces):
+                nc.sync.dma_start(
+                    out=g_chunk[:, i * cols : (i + 1) * cols],
+                    in_=G[
+                        rb * P : (rb + 1) * P,
+                        c * G_CHUNK_COLS + i * cols : c * G_CHUNK_COLS + (i + 1) * cols,
+                    ],
+                )
             g_tiles[n] = g_chunk
 
         def load_x(j):
@@ -116,27 +127,35 @@ def tile_nntransformlearner_pb_k_kernel(tc, G, x_next, out):
                     start=(c == 0 and i == 0),
                     stop=(c == G_CHUNKS - 1 and first + TENSOR_SUM_SLICE == G_CHUNK_COLS),
                 )
-            nc.vector.tensor_scalar(
-                out=g_chunk[:, :split],
-                in0=g_chunk[:, :split],
-                scalar1=1.0,
-                scalar2=None,
-                op0=MULT,
-                op1=ADD,
-                accum_out=partial_sums[:, rb, c : c + 1],
-            )
-            if split < tensor_from:
-                nc.scalar.activation(
-                    out=g_chunk[:, split:tensor_from],
-                    in_=g_chunk[:, split:tensor_from],
-                    func=COPY,
-                    accum_out=partial_sums[:, rb, SUM_SLOTS + c : SUM_SLOTS + c + 1],
+            if n == G_CHUNKS - 1:
+                ranges = [
+                    (i * PIECE_COLS, i * PIECE_COLS + PIECE_VECTOR_COLS, (i + 1) * PIECE_COLS)
+                    for i in range(LAST_PIECES)
+                ]
+            else:
+                ranges = [(0, split, tensor_from)]
+            for i, (first, middle, end) in enumerate(ranges):
+                nc.vector.tensor_scalar(
+                    out=g_chunk[:, first:middle],
+                    in0=g_chunk[:, first:middle],
+                    scalar1=1.0,
+                    scalar2=None,
+                    op0=MULT,
+                    op1=ADD,
+                    accum_out=partial_sums[:, rb, c + i : c + i + 1],
                 )
+                if middle < end:
+                    nc.scalar.activation(
+                        out=g_chunk[:, middle:end],
+                        in_=g_chunk[:, middle:end],
+                        func=COPY,
+                        accum_out=partial_sums[:, rb, SUM_SLOTS + c + i : SUM_SLOTS + c + i + 1],
+                    )
 
         def finish_row_sums(rb):
             if TENSOR_SUM_COLS[rb]:
                 nc.vector.tensor_reduce(
-                    out=partial_sums[:, rb, G_CHUNKS : G_CHUNKS + 1],
+                    out=partial_sums[:, rb, TENSOR_SUM_SLOT : TENSOR_SUM_SLOT + 1],
                     in_=sum_tiles[rb][:],
                     axis=AXIS_X,
                     op=ADD,

@@ -33,7 +33,7 @@ BANKS = G_CHUNK_PASSES // BANK_PASSES
 
 TENSOR_SUM_SLICE = 272
 TENSOR_SUM_COLS = (0, 12 * TENSOR_SUM_SLICE, 0, 0)
-VECTOR_SUM_COLS = (2816, 832, 2688, 2688)
+VECTOR_SUM_COLS = (2816, 832, 2464, 2464)
 SUM_SLOTS = 8
 TENSOR_SUM_SLOT = SUM_SLOTS - 1
 

from contextlib import ExitStack

import concourse.mybir as mybir
from concourse.masks import make_identity

F32 = mybir.dt.float32
BF16 = mybir.dt.bfloat16
U32 = mybir.dt.uint32
U8 = mybir.dt.uint8
FP8X4 = mybir.dt.float8_e4m3fn_x4
MULT = mybir.AluOpType.mult
ADD = mybir.AluOpType.add
COPY = mybir.ActivationFunctionType.Copy
AXIS_X = mybir.AxisListType.X

P = 128
PACK = 4
K_PASS = P * PACK
ROWS, K, D = 512, 16384, 256
ROW_BLOCKS = ROWS // P
PASSES = K // K_PASS

G_CHUNK_PASSES = 8
G_CHUNK_COLS = G_CHUNK_PASSES * K_PASS
G_CHUNKS = K // G_CHUNK_COLS
X_CHUNK_PASSES = 4
X_CHUNKS = PASSES // X_CHUNK_PASSES
BANK_PASSES = 2
BANK_WORDS = 512

CHUNKS = ROW_BLOCKS * G_CHUNKS
BANKS = G_CHUNK_PASSES // BANK_PASSES

TENSOR_SUM_SLICE = 272
TENSOR_SUM_COLS = (0, 12 * TENSOR_SUM_SLICE, 0, 0)
VECTOR_SUM_COLS = (2816, 832, 2464, 2464)
SUM_SLOTS = 8
TENSOR_SUM_SLOT = SUM_SLOTS - 1

LAST_PIECES = 4
PIECE_COLS = G_CHUNK_COLS // LAST_PIECES
PIECE_VECTOR_COLS = 704

LOAD_LEAD = 6
SUM_LEAD = 5
X_CHUNKS_A_STEP = 2
X_STEPS = X_CHUNKS // X_CHUNKS_A_STEP
X_FIRST_STEP = -1
SCALAR_X_PASSES = 2

FLOPS = 2 * ROWS * K * D


def tile_nntransformlearner_pb_k_kernel(tc, G, x_next, out):
    nc = tc.nc
    with ExitStack() as stack:
        const = stack.enter_context(tc.tile_pool(name="const", bufs=1))
        g_pool = stack.enter_context(tc.tile_pool(name="g", bufs=12))
        x_raw_pool = stack.enter_context(tc.tile_pool(name="x_raw", bufs=4))
        x_grouped_pool = stack.enter_context(tc.tile_pool(name="x_grouped", bufs=2))
        p_grouped_pool = stack.enter_context(tc.tile_pool(name="p_grouped", bufs=3))
        p_mx_pool = stack.enter_context(tc.tile_pool(name="p_mx", bufs=3))
        result_pool = stack.enter_context(tc.tile_pool(name="result", bufs=2))
        turned_pool = stack.enter_context(tc.psum_pool(name="turned", bufs=5))
        sum_pool = stack.enter_context(tc.psum_pool(name="sums", bufs=1))
        acc_pool = stack.enter_context(tc.psum_pool(name="acc", bufs=2))
        stack.enter_context(tc.manual_schedule())

        identity = const.tile([P, P], F32, name="identity")
        make_identity(nc, identity[:])
        identity_bf16 = const.tile([P, P], BF16, name="identity_bf16")
        make_identity(nc, identity_bf16[:])
        partial_sums = const.tile([P, ROW_BLOCKS, 2 * SUM_SLOTS], F32, name="partial_sums")
        nc.vector.memset(partial_sums[:], 0.0)
        row_sum = const.tile([P, ROW_BLOCKS], F32, name="row_sum")
        row_scale = const.tile([P, ROW_BLOCKS], F32, name="row_scale")
        x_codes = const.tile([P, PASSES * D], U32, name="x_codes", align_bytes=64)
        x_scales = const.tile([P, PASSES * D], U8, name="x_scales", align_bytes=64)

        x_view = x_next.rearrange("(c q e) d -> q c (e d)", q=P, e=2)
        g_tiles = {}
        x_raw_tiles = {}
        x_grouped_tiles = {}
        turned_tiles = {}
        p_grouped_tiles = {}
        p_mx_tiles = {}
        acc_tiles = {}
        sum_tiles = {}

        def load_g(n):
            rb, c = divmod(n, G_CHUNKS)
            g_chunk = g_pool.tile([P, G_CHUNK_COLS], BF16, name="g_chunk")
            pieces = LAST_PIECES if n == G_CHUNKS - 1 else 1
            cols = G_CHUNK_COLS // pieces
            for i in range(pieces):
                nc.sync.dma_start(
                    out=g_chunk[:, i * cols : (i + 1) * cols],
                    in_=G[
                        rb * P : (rb + 1) * P,
                        c * G_CHUNK_COLS + i * cols : c * G_CHUNK_COLS + (i + 1) * cols,
                    ],
                )
            g_tiles[n] = g_chunk

        def load_x(j):
            x_raw = x_raw_pool.tile([P, X_CHUNK_PASSES * PACK * D], BF16, name="x_raw")
            halves = 2 * X_CHUNK_PASSES
            nc.sync.dma_start(
                out=x_raw[:].rearrange("p (c r) -> p c r", c=halves),
                in_=x_view[:, j * halves : (j + 1) * halves, :],
            )
            x_raw_tiles[j] = x_raw

        def sum_rows(n):
            rb, c = divmod(n, G_CHUNKS)
            g_chunk = g_tiles[n]
            split = VECTOR_SUM_COLS[rb]
            tensor_from = G_CHUNK_COLS - TENSOR_SUM_COLS[rb]
            if c == 0 and TENSOR_SUM_COLS[rb]:
                sum_tiles[rb] = sum_pool.tile([P, TENSOR_SUM_SLICE], F32, name="slice_sums")
            for i in range(TENSOR_SUM_COLS[rb] // TENSOR_SUM_SLICE):
                first = tensor_from + i * TENSOR_SUM_SLICE
                nc.tensor.matmul(
                    out=sum_tiles[rb][:],
                    lhsT=identity_bf16[:],
                    rhs=g_chunk[:, first : first + TENSOR_SUM_SLICE],
                    start=(c == 0 and i == 0),
                    stop=(c == G_CHUNKS - 1 and first + TENSOR_SUM_SLICE == G_CHUNK_COLS),
                )
            if n == G_CHUNKS - 1:
                ranges = [
                    (i * PIECE_COLS, i * PIECE_COLS + PIECE_VECTOR_COLS, (i + 1) * PIECE_COLS)
                    for i in range(LAST_PIECES)
                ]
            else:
                ranges = [(0, split, tensor_from)]
            for i, (first, middle, end) in enumerate(ranges):
                nc.vector.tensor_scalar(
                    out=g_chunk[:, first:middle],
                    in0=g_chunk[:, first:middle],
                    scalar1=1.0,
                    scalar2=None,
                    op0=MULT,
                    op1=ADD,
                    accum_out=partial_sums[:, rb, c + i : c + i + 1],
                )
                if middle < end:
                    nc.scalar.activation(
                        out=g_chunk[:, middle:end],
                        in_=g_chunk[:, middle:end],
                        func=COPY,
                        accum_out=partial_sums[:, rb, SUM_SLOTS + c + i : SUM_SLOTS + c + i + 1],
                    )

        def finish_row_sums(rb):
            if TENSOR_SUM_COLS[rb]:
                nc.vector.tensor_reduce(
                    out=partial_sums[:, rb, TENSOR_SUM_SLOT : TENSOR_SUM_SLOT + 1],
                    in_=sum_tiles[rb][:],
                    axis=AXIS_X,
                    op=ADD,
                )
            nc.vector.tensor_reduce(
                out=row_sum[:, rb : rb + 1], in_=partial_sums[:, rb, :], axis=AXIS_X, op=ADD
            )
            nc.vector.reciprocal(out=row_scale[:, rb : rb + 1], in_=row_sum[:, rb : rb + 1])

        def regroup_x(j, scalar_passes):
            x_grouped = x_grouped_pool.tile(
                [P, X_CHUNK_PASSES * D * PACK], BF16, name="x_grouped", align_bytes=64
            )
            to = x_grouped[:].rearrange("p (g c i t) -> p g c t i", g=X_CHUNK_PASSES, i=4, t=PACK)
            of = x_raw_tiles[j][:].rearrange(
                "p (g t c i) -> p g c t i", g=X_CHUNK_PASSES, i=4, t=PACK
            )
            vector_passes = X_CHUNK_PASSES - scalar_passes
            nc.vector.tensor_copy(out=to[:, :vector_passes], in_=of[:, :vector_passes])
            for g in range(vector_passes, X_CHUNK_PASSES):
                nc.scalar.copy(out=to[:, g], in_=of[:, g])
            x_grouped_tiles[j] = x_grouped

        def quantise_x(j):
            cols = slice(j * X_CHUNK_PASSES * D, (j + 1) * X_CHUNK_PASSES * D)
            nc.vector.quantize_mx(
                out=x_codes[:, cols].bitcast(FP8X4),
                scales=x_scales[:, cols],
                in_=x_grouped_tiles[j][:],
            )

        def scale_rows(n):
            g_chunk = g_tiles[n]
            rb = n // G_CHUNKS
            nc.vector.tensor_scalar(
                out=g_chunk[:],
                in0=g_chunk[:],
                scalar1=row_scale[:, rb : rb + 1],
                scalar2=None,
                op0=MULT,
            )

        def transpose_bank(n, b):
            p_words = g_tiles[n][:].bitcast(F32)
            turned = turned_pool.tile([P, BANK_WORDS], F32, name="turned")
            for s in range(BANK_WORDS // P):
                w = b * BANK_WORDS + s * P
                nc.tensor.transpose(
                    out=turned[:, s * P : (s + 1) * P],
                    in_=p_words[:, w : w + P],
                    identity=identity[:],
                )
            turned_tiles[(n, b)] = turned

        def copy_bank(n, b):
            if b == 0:
                p_grouped_tiles[n] = p_grouped_pool.tile(
                    [P, G_CHUNK_COLS], BF16, name="p_grouped", align_bytes=64
                )
            p_grouped_words = p_grouped_tiles[n][:].bitcast(F32).rearrange(
                "p (g m u) -> p g m u", g=G_CHUNK_PASSES, u=2
            )
            nc.scalar.copy(
                out=p_grouped_words[:, b * BANK_PASSES : (b + 1) * BANK_PASSES, :, :],
                in_=turned_tiles[(n, b)][:].rearrange("p (g u m) -> p g m u", g=BANK_PASSES, u=2),
            )

        def quantise_p(n):
            p_codes = p_mx_pool.tile([P, G_CHUNK_PASSES * P], U32, name="p_codes", align_bytes=64)
            p_scales = p_mx_pool.tile([P, G_CHUNK_PASSES * P], U8, name="p_scales", align_bytes=64)
            nc.vector.quantize_mx(
                out=p_codes[:].bitcast(FP8X4), scales=p_scales[:], in_=p_grouped_tiles[n][:]
            )
            p_mx_tiles[n] = (p_codes, p_scales)

        def multiply(n):
            rb, c = divmod(n, G_CHUNKS)
            if c == 0:
                acc_tiles[rb] = acc_pool.tile([P, D], F32, name="acc")
            acc = acc_tiles[rb]
            p_codes, p_scales = p_mx_tiles[n]
            for i in range(G_CHUNK_PASSES):
                g = c * G_CHUNK_PASSES + i
                nc.tensor.matmul_mx(
                    out=acc[:],
                    lhsT=p_codes[:, i * P : (i + 1) * P].bitcast(FP8X4),
                    lhsT_scale=p_scales[:, i * P : (i + 1) * P],
                    rhs=x_codes[:, g * D : (g + 1) * D].bitcast(FP8X4),
                    rhs_scale=x_scales[:, g * D : (g + 1) * D],
                    start=(g == 0),
                    stop=(g == PASSES - 1),
                )

        def store(rb):
            result = result_pool.tile([P, D], F32, name="result")
            nc.scalar.copy(out=result[:], in_=acc_tiles[rb][:])
            nc.sync.dma_start(out=out[rb * P : (rb + 1) * P, :], in_=result[:])

        for s in range(-LOAD_LEAD, CHUNKS + 3):
            xs = s - X_FIRST_STEP
            prepares_x = 0 <= xs < X_STEPS
            if 0 <= xs + 1 < X_STEPS:
                load_x(X_CHUNKS_A_STEP * (xs + 1))
                load_x(X_CHUNKS_A_STEP * (xs + 1) + 1)
            if s + LOAD_LEAD < CHUNKS:
                load_g(s + LOAD_LEAD)
            if (s + 1) % G_CHUNKS == 0 and 0 <= s + 1 < CHUNKS:
                finish_row_sums((s + 1) // G_CHUNKS)
            if 0 <= s + 1 < CHUNKS:
                scale_rows(s + 1)
            if 0 <= s - 2 < CHUNKS:
                multiply(s - 2)
            for b in range(BANKS):
                if 0 <= s < CHUNKS:
                    copy_bank(s, b)
                if 0 <= s + 1 < CHUNKS:
                    transpose_bank(s + 1, b)
            if prepares_x:
                regroup_x(X_CHUNKS_A_STEP * xs, SCALAR_X_PASSES)
            if 0 <= s - 1 < CHUNKS:
                quantise_p(s - 1)
            if prepares_x:
                regroup_x(X_CHUNKS_A_STEP * xs + 1, SCALAR_X_PASSES)
                quantise_x(X_CHUNKS_A_STEP * xs)
            if 0 <= s + SUM_LEAD < CHUNKS:
                sum_rows(s + SUM_LEAD)
            if prepares_x:
                quantise_x(X_CHUNKS_A_STEP * xs + 1)
            if (s - 2) % G_CHUNKS == G_CHUNKS - 1 and 0 <= s - 2 < CHUNKS:
                store((s - 2) // G_CHUNKS)
